import numpy as np
import ml_dtypes


def mxq(x, axis, fmt="e4m3"):
    dtype, down = {"e4m3": (ml_dtypes.float8_e4m3fn, 7), "e5m2": (ml_dtypes.float8_e5m2, 14)}[fmt]
    v = np.moveaxis(np.asarray(x, np.float32).astype(ml_dtypes.bfloat16).astype(np.float64), axis, -1)
    blocks = v.reshape(v.shape[:-1] + (-1, 32))
    amax = np.abs(blocks).max(-1, keepdims=True)
    byte = np.maximum(np.where(amax > 0, np.frexp(amax)[1] - 1 + 127, 0) - down, 1)
    scale = np.exp2(byte - 127.0)
    codes = (blocks / scale).astype(np.float32).astype(dtype).astype(np.float64)
    return np.moveaxis((codes * scale).reshape(v.shape), -1, axis)


WIDE = False


def mx_kscale(k):
    if not WIDE:
        return np.ones(k)
    levels = np.array([10, -10, 5, -5, 0])
    if k % 512:
        return np.exp2(np.random.permutation(np.resize(levels, k // 32))).repeat(32)
    a = np.empty((k // 512, 16))
    for p in range(k // 512):
        a[p, :8] = np.random.permutation(np.resize(levels, 8))
        for g in range(8):
            far = levels[np.abs(levels - a[p, g]) >= 10]
            a[p, g + 8] = far[np.random.randint(len(far))]
    return np.exp2(a.ravel()).repeat(32)


BF16 = ml_dtypes.bfloat16


def bf(x):
    return np.asarray(x, np.float32).astype(BF16)


def f64(x):
    return np.asarray(x).astype(np.float64)


B, T, C, H, KV, HD = 2, 256, 2048, 16, 4, 128
NQ = H * HD
NK = KV * HD
HALF = HD // 2
ROPE_THETA = 10000.0


def apply_rope(u, cos, sin):
    ur = u.reshape(*u.shape[:-1], HALF, 2)
    ue, uo = ur[..., 0], ur[..., 1]
    c = cos[None, :, None, :]
    s = sin[None, :, None, :]
    out_e = ue * c - uo * s
    out_o = ue * s + uo * c
    return np.stack([out_e, out_o], axis=-1).reshape(u.shape)


def draw0():
    s = mx_kscale(C)
    inv_freq = 1.0 / ROPE_THETA ** (np.arange(0, HD, 2) / HD)
    angles = np.arange(T)[:, None] * inv_freq[None, :]
    return {"x": bf(np.random.standard_normal((B, T, C)) * s),
            "w_qkv": bf(np.random.standard_normal((NQ + NK + NK, C)) / np.sqrt(C) / s[None, :]),
            "freqs_cos": bf(np.cos(angles)),
            "freqs_sin": bf(np.sin(angles))}


def core(x, w_qkv, freqs_cos, freqs_sin):
    cos, sin = f64(freqs_cos), f64(freqs_sin)
    qkv = mxq(f64(x), 2, "e4m3") @ mxq(f64(w_qkv), 1, "e4m3").T
    q = qkv[..., :NQ].reshape(B, T, H, HD)
    k = qkv[..., NQ:NQ + NK].reshape(B, T, KV, HD)
    v = qkv[..., NQ + NK:].reshape(B, T, KV, HD)
    return apply_rope(q, cos, sin), apply_rope(k, cos, sin), v


def e4m3fn_bytes(y):
    return np.clip(np.asarray(y, np.float64), -448.0, 448.0).astype(np.float32).astype(ml_dtypes.float8_e4m3fn).view(np.uint8)


def e4m3fn_values(b):
    return np.asarray(b, np.uint8).view(ml_dtypes.float8_e4m3fn).astype(np.float64)


def setup_inputs():
    d = draw0()
    x0 = np.asarray(d['w_qkv']).astype(np.float64)
    s = (np.max(np.abs(x0), axis=(0,), keepdims=True) / 448.0).astype(np.float32)
    out = {}
    for k, v in d.items():
        if k == 'w_qkv':
            out['w_qkv_bytes'] = e4m3fn_bytes(x0 / s.astype(np.float64))
            out['w_qkv_scale'] = s
        else:
            out[k] = v
    return out


def reference(x, w_qkv_bytes, w_qkv_scale, freqs_cos, freqs_sin):
    return core(x, e4m3fn_values(w_qkv_bytes) * w_qkv_scale.astype(np.float64), freqs_cos, freqs_sin)

@@ -1,0 +1,285 @@
+from contextlib import ExitStack
+
+import concourse.mybir as mybir
+from concourse.masks import make_identity
+
+FLOPS = 2 * 512 * 2048 * 3072
+
+F32 = mybir.dt.float32
+BF16 = mybir.dt.bfloat16
+U32 = mybir.dt.uint32
+U8 = mybir.dt.uint8
+FP8 = mybir.dt.float8_e4m3fn
+FP8X4 = mybir.dt.float8_e4m3fn_x4
+MULT = mybir.AluOpType.mult
+ADD = mybir.AluOpType.add
+
+P = 128
+UNITS = 24
+ROPE_BANKS = 20
+LAG = 5
+
+
+def tile_causalselfattention_pa_kernel(
+    tc, x, w_qkv_bytes, w_qkv_scale, freqs_cos, freqs_sin, out_0, out_1, out_2
+):
+    nc = tc.nc
+    x_rows = x.flatten_outer_dims()
+    out_rows = [
+        out_0.rearrange("b t h d -> (b t) (h d)"),
+        out_1.rearrange("b t h d -> (b t) (h d)"),
+        out_2.rearrange("b t h d -> (b t) (h d)"),
+    ]
+
+    with ExitStack() as ctx:
+        const = ctx.enter_context(tc.tile_pool(name="const", bufs=1))
+        ring = ctx.enter_context(tc.tile_pool(name="ring", bufs=4))
+        psum = ctx.enter_context(tc.psum_pool(name="psum", bufs=4))
+        ctx.enter_context(tc.manual_schedule())
+
+        scale_sb = const.tile([P, 16], F32, name="scale_sb")
+        nc.scalar.dma_start(
+            out=scale_sb[:].rearrange("p (g t) -> p g t", t=4),
+            in_=w_qkv_scale.rearrange("o (g p t) -> p (o g) t", p=P, t=4),
+        )
+        cos_raw = const.tile([P, 2, 64], BF16, name="cos_raw")
+        nc.scalar.dma_start(out=cos_raw[:], in_=freqs_cos.rearrange("(th p) j -> p th j", p=P))
+        sin_raw = const.tile([P, 2, 64], BF16, name="sin_raw")
+        nc.scalar.dma_start(out=sin_raw[:], in_=freqs_sin.rearrange("(th p) j -> p th j", p=P))
+
+        warm_in = const.tile([P, 1], F32, name="warm_in")
+        warm_out = const.tile([P, 1], F32, name="warm_out")
+        nc.gpsimd.memset(warm_in[:], 0.0)
+        nc.scalar.copy(out=warm_out[:], in_=warm_in[:])
+
+        ident = const.tile([P, P], F32, name="ident")
+        make_identity(nc, ident[:])
+
+        wq = {}
+        xs = {}
+
+        def load_w(j):
+            i, g = j // 4, j % 4
+            wq[j] = const.tile([P, 4, 512], U8, name="wq%d" % j)
+            nc.sync.dma_start(
+                out=wq[j][:],
+                in_=w_qkv_bytes[512 * i : 512 * (i + 1), 512 * g : 512 * (g + 1)].rearrange(
+                    "(a p) k -> p a k", p=P
+                ),
+            )
+
+        def load_x(g):
+            xs[g] = const.tile([P, 4, 512], BF16, name="xs%d" % g)
+            nc.sync.dma_start(
+                out=xs[g][:],
+                in_=x_rows[:, 512 * g : 512 * (g + 1)].rearrange("(m p) k -> p m k", p=P),
+            )
+
+        load_w(0)
+        load_w(1)
+        for g in range(4):
+            load_x(g)
+            load_w(g + 2)
+        for j in range(6, UNITS):
+            load_w(j)
+
+        cos2 = const.tile([P, 2, 64, 2], F32, name="cos2")
+        sin2 = const.tile([P, 2, 64, 2], F32, name="sin2")
+        nc.gpsimd.tensor_copy(out=cos2[:, :, :, 0], in_=cos_raw[:])
+        nc.gpsimd.tensor_copy(out=cos2[:, :, :, 1], in_=cos_raw[:])
+        nc.gpsimd.tensor_scalar(out=sin2[:, :, :, 0], in0=sin_raw[:], scalar1=-1.0, scalar2=None, op0=MULT)
+        nc.gpsimd.tensor_copy(out=sin2[:, :, :, 1], in_=sin_raw[:])
+
+        xg = [const.tile([P, 2048], BF16, name="xg%d" % g, align_bytes=64) for g in range(4)]
+        xc = [const.tile([P, 512], U32, name="xc%d" % g, align_bytes=64) for g in range(4)]
+        xsc = [const.tile([P, 512], U8, name="xsc%d" % g, align_bytes=64) for g in range(4)]
+
+        wb = {}
+        tp = {}
+        xt = {}
+        wg = {}
+        wc = {}
+        ws = {}
+        acc = {}
+        u_sb = {}
+        a_sb = {}
+        s_sb = {}
+
+        def cast(j):
+            wb[j] = ring.tile([P, 2048], BF16, name="wb", tag="wb", bufs=6)
+            flat = wq[j][:].rearrange("p a k -> p (a k)")
+            for h in range(2):
+                nc.scalar.copy(
+                    out=wb[j][:, 1024 * h : 1024 * (h + 1)],
+                    in_=flat[:, 1024 * h : 1024 * (h + 1)].bitcast(FP8),
+                )
+
+        def turn(words, bank, h):
+            for u in range(2):
+                for a2 in range(2):
+                    a = 2 * h + a2
+                    nc.tensor.transpose(
+                        bank[:, u, 128 * a2 : 128 * (a2 + 1)],
+                        words[:, 256 * a + u : 256 * (a + 1) : 2],
+                        ident[:],
+                    )
+
+        def transposes(j, h):
+            tp[(j, h)] = psum.tile([P, 2, 256], F32, name="tp", tag="tp")
+            turn(wb[j][:].bitcast(F32), tp[(j, h)], h)
+
+        def x_transposes(g):
+            words = xs[g][:].rearrange("p m k -> p (m k)").bitcast(F32)
+            for h in range(2):
+                xt[(g, h)] = psum.tile([P, 2, 256], F32, name="xt", tag="acc")
+                turn(words, xt[(g, h)], h)
+
+        def x_out(g, h):
+            nc.scalar.copy(
+                out=xg[g][:, 1024 * h : 1024 * (h + 1)].bitcast(F32).rearrange("p (r u) -> p r u", u=2),
+                in_=xt[(g, h)][:].rearrange("p u r -> p r u"),
+            )
+
+        def x_quant(g):
+            nc.vector.quantize_mx(out=xc[g][:].bitcast(FP8X4), scales=xsc[g][:], in_=xg[g][:])
+
+        def scale_half(j, h):
+            g = j % 4
+            if h == 0:
+                wg[j] = ring.tile([P, 2048], BF16, name="wg", tag="wg%d" % (j % 3), bufs=1, align_bytes=64)
+            nc.vector.tensor_tensor(
+                out=wg[j][:, 1024 * h : 1024 * (h + 1)].rearrange("p (r u e) -> p r u e", u=2, e=2),
+                in0=tp[(j, h)][:]
+                .rearrange("p u r -> p (u r)")
+                .bitcast(BF16)
+                .rearrange("p (u r e) -> p r u e", u=2, e=2),
+                in1=scale_sb[:, 4 * g : 4 * g + 4]
+                .rearrange("p (o u e) -> p o u e", o=1, u=2, e=2)
+                .to_broadcast([P, 256, 2, 2]),
+                op=MULT,
+            )
+
+        def quant(j):
+            wc[j] = ring.tile([P, 512], U32, name="wc", tag="wc", bufs=8, align_bytes=64)
+            ws[j] = ring.tile([P, 512], U8, name="ws", tag="ws", bufs=8, align_bytes=64)
+            nc.vector.quantize_mx(out=wc[j][:].bitcast(FP8X4), scales=ws[j][:], in_=wg[j][:])
+
+        def new_bank(b, tag):
+            acc[b] = psum.tile([P, 512], F32, name="acc", tag=tag)
+
+        def passes(b, gs):
+            i, m = b // 4, b % 4
+            for g in gs:
+                nc.tensor.matmul_mx(
+                    out=acc[b][:],
+                    lhsT=xc[g][:, 128 * m : 128 * (m + 1)].bitcast(FP8X4),
+                    lhsT_scale=xsc[g][:, 128 * m : 128 * (m + 1)],
+                    rhs=wc[4 * i + g][:].bitcast(FP8X4),
+                    rhs_scale=ws[4 * i + g][:],
+                    start=(g == 0),
+                    stop=(g == 3),
+                )
+
+        def store(b, tile_ap):
+            i, m = b // 4, b % 4
+            dst = out_rows[0] if i < 4 else out_rows[i - 3]
+            c0 = 512 * i if i < 4 else 0
+            nc.sync.dma_start(out=dst[128 * m : 128 * (m + 1), c0 : c0 + 512], in_=tile_ap)
+
+        def heads(ap):
+            return ap.rearrange("p (h j e) -> p h j e", h=4, e=2)
+
+        def table(t, b):
+            return t[:, b % 2, :, :].unsqueeze(1).to_broadcast([P, 4, 64, 2])
+
+        def copy_u(b):
+            u_sb[b] = ring.tile([P, 512], F32, name="u_sb", tag="u_sb")
+            nc.scalar.copy(out=u_sb[b][:], in_=acc[b][:])
+
+        def rope_cos(b):
+            a_sb[b] = ring.tile([P, 512], F32, name="a_sb", tag="a_sb")
+            nc.vector.tensor_tensor(out=heads(a_sb[b][:]), in0=heads(acc[b][:]), in1=table(cos2, b), op=MULT)
+
+        def rope_sin(b):
+            s_sb[b] = ring.tile([P, 512], F32, name="s_sb", tag="wg%d" % ((b + LAG - 1) % 3), bufs=1, align_bytes=64)
+            nc.gpsimd.tensor_tensor(
+                out=heads(s_sb[b][:]), in0=heads(u_sb[b][:])[:, :, :, ::-1], in1=table(sin2, b), op=MULT
+            )
+
+        def rope_sin_on_vector(b):
+            s_sb[b] = ring.tile([P, 512], F32, name="s_v", tag="s_v", bufs=1)
+            nc.vector.tensor_tensor(
+                out=heads(s_sb[b][:]), in0=heads(acc[b][:])[:, :, :, ::-1], in1=table(sin2, b), op=MULT
+            )
+
+        def rope_add(b, eng):
+            o_sb = ring.tile([P, 512], F32, name="o_sb", tag="o_sb", bufs=8)
+            eng.tensor_tensor(out=o_sb[:], in0=a_sb[b][:], in1=s_sb[b][:], op=ADD)
+            store(b, o_sb[:])
+
+        def plain_out(b, on_scalar):
+            o_sb = ring.tile([P, 512], F32, name="o_sb", tag="o_sb", bufs=8)
+            if on_scalar:
+                nc.scalar.copy(out=o_sb[:], in_=acc[b][:])
+            else:
+                nc.vector.tensor_copy(out=o_sb[:], in_=acc[b][:])
+            store(b, o_sb[:])
+
+        cast(0)
+        cast(1)
+        casts_done = 2
+        transposes(0, 0)
+        transposes(0, 1)
+        for s in range(UNITS):
+            b = s - LAG
+            early = 0 <= b < ROPE_BANKS - 2
+            if s < 4:
+                x_transposes(s)
+            if early:
+                new_bank(b, "acc")
+            for h in range(2):
+                if early:
+                    passes(b, (2 * h, 2 * h + 1))
+                if s + 1 < UNITS:
+                    transposes(s + 1, h)
+            if s < 4:
+                x_out(s, 0)
+                x_out(s, 1)
+            if early:
+                copy_u(b)
+            lead = 2 if s < 4 else 3
+            while casts_done <= min(s + lead, UNITS - 1):
+                cast(casts_done)
+                casts_done += 1
+            scale_half(s, 0)
+            if s >= 1:
+                quant(s - 1)
+            if 1 <= s <= 4:
+                x_quant(s - 1)
+            if 0 <= b and s < UNITS - 1:
+                rope_cos(b)
+            scale_half(s, 1)
+            if s == UNITS - 1:
+                quant(s)
+                rope_cos(b)
+            if 0 <= b:
+                rope_sin(b)
+                rope_add(b, nc.gpsimd)
+            if s == UNITS - 2:
+                for bb in (ROPE_BANKS - 2, ROPE_BANKS - 1):
+                    new_bank(bb, "acc")
+                    passes(bb, (0, 1, 2, 3))
+                copy_u(ROPE_BANKS - 2)
+                for m in range(4):
+                    new_bank(ROPE_BANKS + m, "acc" if m < 2 else "tp")
+                    passes(ROPE_BANKS + m, (0, 1))
+            if s == UNITS - 1:
+                for m in range(4):
+                    passes(ROPE_BANKS + m, (2,))
+        for m in range(4):
+            passes(ROPE_BANKS + m, (3,))
+        rope_cos(ROPE_BANKS - 1)
+        rope_sin_on_vector(ROPE_BANKS - 1)
+        for m in range(4):
+            plain_out(ROPE_BANKS + m, True)
+        rope_add(ROPE_BANKS - 1, nc.vector)

@@ -17,7 +17,8 @@ ADD = mybir.AluOpType.add
 P = 128
 UNITS = 24
 ROPE_BANKS = 20
-LAG = 5
+PE_LAG = 4
+PAIR_LAG = 3
 
 
 def tile_causalselfattention_pa_kernel(
@@ -90,6 +91,16 @@ def tile_causalselfattention_pa_kernel(
         nc.gpsimd.tensor_scalar(out=sin2[:, :, :, 0], in0=sin_raw[:], scalar1=-1.0, scalar2=None, op0=MULT)
         nc.gpsimd.tensor_copy(out=sin2[:, :, :, 1], in_=sin_raw[:])
 
+        sin_full = const.tile([P, 1024], F32, name="sin_full")
+        nc.gpsimd.tensor_scalar(
+            out=sin_full[:].rearrange("p (t h n) -> p t h n", t=2, h=4),
+            in0=sin2[:].rearrange("p t j e -> p t (j e)").unsqueeze(2).to_broadcast([P, 2, 4, 128]),
+            scalar1=1.0,
+            scalar2=0.0,
+            op0=MULT,
+            op1=ADD,
+        )
+
         xg = [const.tile([P, 2048], BF16, name="xg%d" % g, align_bytes=64) for g in range(4)]
         xc = [const.tile([P, 512], U32, name="xc%d" % g, align_bytes=64) for g in range(4)]
         xsc = [const.tile([P, 512], U8, name="xsc%d" % g, align_bytes=64) for g in range(4)]
@@ -145,10 +156,12 @@ def tile_causalselfattention_pa_kernel(
 
         def scale_half(j, h):
             g = j % 4
-            if h == 0:
-                wg[j] = ring.tile([P, 2048], BF16, name="wg", tag="wg%d" % (j % 3), bufs=1, align_bytes=64)
+            k, q = j // 2, j % 2
+            if q == 0 and h == 0:
+                wg[k] = ring.tile([P, 4096], BF16, name="wg", tag="wg%d" % (k % 3), bufs=1, align_bytes=64)
+            c0 = 2048 * q + 1024 * h
             nc.vector.tensor_tensor(
-                out=wg[j][:, 1024 * h : 1024 * (h + 1)].rearrange("p (r u e) -> p r u e", u=2, e=2),
+                out=wg[k][:, c0 : c0 + 1024].rearrange("p (r u e) -> p r u e", u=2, e=2),
                 in0=tp[(j, h)][:]
                 .rearrange("p u r -> p (u r)")
                 .bitcast(BF16)
@@ -159,10 +172,10 @@ def tile_causalselfattention_pa_kernel(
                 op=MULT,
             )
 
-        def quant(j):
-            wc[j] = ring.tile([P, 512], U32, name="wc", tag="wc", bufs=8, align_bytes=64)
-            ws[j] = ring.tile([P, 512], U8, name="ws", tag="ws", bufs=8, align_bytes=64)
-            nc.vector.quantize_mx(out=wc[j][:].bitcast(FP8X4), scales=ws[j][:], in_=wg[j][:])
+        def quant(k):
+            wc[k] = ring.tile([P, 1024], U32, name="wc", tag="wc", bufs=4, align_bytes=64)
+            ws[k] = ring.tile([P, 1024], U8, name="ws", tag="ws", bufs=4, align_bytes=64)
+            nc.vector.quantize_mx(out=wc[k][:].bitcast(FP8X4), scales=ws[k][:], in_=wg[k][:])
 
         def new_bank(b, tag):
             acc[b] = psum.tile([P, 512], F32, name="acc", tag=tag)
@@ -170,60 +183,82 @@ def tile_causalselfattention_pa_kernel(
         def passes(b, gs):
             i, m = b // 4, b % 4
             for g in gs:
+                j = 4 * i + g
+                cols = slice(512 * (j % 2), 512 * (j % 2 + 1))
                 nc.tensor.matmul_mx(
                     out=acc[b][:],
                     lhsT=xc[g][:, 128 * m : 128 * (m + 1)].bitcast(FP8X4),
                     lhsT_scale=xsc[g][:, 128 * m : 128 * (m + 1)],
-                    rhs=wc[4 * i + g][:].bitcast(FP8X4),
-                    rhs_scale=ws[4 * i + g][:],
+                    rhs=wc[j // 2][:, cols].bitcast(FP8X4),
+                    rhs_scale=ws[j // 2][:, cols],
                     start=(g == 0),
                     stop=(g == 3),
                 )
 
-        def store(b, tile_ap):
-            i, m = b // 4, b % 4
+        def out_view(b):
+            i = b // 4
             dst = out_rows[0] if i < 4 else out_rows[i - 3]
             c0 = 512 * i if i < 4 else 0
-            nc.sync.dma_start(out=dst[128 * m : 128 * (m + 1), c0 : c0 + 512], in_=tile_ap)
+            return dst[:, c0 : c0 + 512]
+
+        def store(b, tile_ap):
+            m = b % 4
+            nc.sync.dma_start(out=out_view(b)[128 * m : 128 * (m + 1), :], in_=tile_ap)
+
+        def store_pair(p, tile_ap):
+            m = (2 * p) % 4
+            nc.sync.dma_start(
+                out=out_view(2 * p)[128 * m : 128 * (m + 2), :].rearrange("(t p) c -> p t c", p=P),
+                in_=tile_ap.rearrange("p (t c) -> p t c", t=2),
+            )
 
         def heads(ap):
             return ap.rearrange("p (h j e) -> p h j e", h=4, e=2)
 
+        def pairs(ap):
+            return ap.rearrange("p (n e) -> p n e", e=2)
+
         def table(t, b):
             return t[:, b % 2, :, :].unsqueeze(1).to_broadcast([P, 4, 64, 2])
 
+        def half(t, b):
+            return t[:, 512 * (b % 2) : 512 * (b % 2 + 1)]
+
         def copy_u(b):
-            u_sb[b] = ring.tile([P, 512], F32, name="u_sb", tag="u_sb")
-            nc.scalar.copy(out=u_sb[b][:], in_=acc[b][:])
+            if b % 2 == 0:
+                u_sb[b // 2] = ring.tile([P, 1024], F32, name="u_sb", tag="u_sb", bufs=3)
+            nc.scalar.copy(out=half(u_sb[b // 2], b), in_=acc[b][:])
 
         def rope_cos(b):
-            a_sb[b] = ring.tile([P, 512], F32, name="a_sb", tag="a_sb")
-            nc.vector.tensor_tensor(out=heads(a_sb[b][:]), in0=heads(acc[b][:]), in1=table(cos2, b), op=MULT)
+            if b % 2 == 0:
+                a_sb[b // 2] = ring.tile([P, 1024], F32, name="a_sb", tag="a_sb", bufs=3)
+            nc.vector.tensor_tensor(out=heads(half(a_sb[b // 2], b)), in0=heads(acc[b][:]), in1=table(cos2, b), op=MULT)
 
-        def rope_sin(b):
-            s_sb[b] = ring.tile([P, 512], F32, name="s_sb", tag="wg%d" % ((b + LAG - 1) % 3), bufs=1, align_bytes=64)
+        def rope_sin(p, k):
+            s_sb[p] = ring.tile([P, 1024], F32, name="s_sb", tag="wg%d" % ((k - 1) % 3), bufs=1, align_bytes=64)
             nc.gpsimd.tensor_tensor(
-                out=heads(s_sb[b][:]), in0=heads(u_sb[b][:])[:, :, :, ::-1], in1=table(sin2, b), op=MULT
+                out=pairs(s_sb[p][:]), in0=pairs(u_sb[p][:])[:, :, ::-1], in1=pairs(sin_full[:]), op=MULT
             )
 
-        def rope_sin_on_vector(b):
-            s_sb[b] = ring.tile([P, 512], F32, name="s_v", tag="s_v", bufs=1)
-            nc.vector.tensor_tensor(
-                out=heads(s_sb[b][:]), in0=heads(acc[b][:])[:, :, :, ::-1], in1=table(sin2, b), op=MULT
-            )
+        def rope_add(p):
+            o_sb = ring.tile([P, 1024], F32, name="o_sb", tag="o_sb", bufs=4)
+            nc.gpsimd.tensor_tensor(out=o_sb[:], in0=a_sb[p][:], in1=s_sb[p][:], op=ADD)
+            store_pair(p, o_sb[:])
 
-        def rope_add(b, eng):
-            o_sb = ring.tile([P, 512], F32, name="o_sb", tag="o_sb", bufs=8)
-            eng.tensor_tensor(out=o_sb[:], in0=a_sb[b][:], in1=s_sb[b][:], op=ADD)
-            store(b, o_sb[:])
+        def rope_rest_on_vector(p):
+            s_v = ring.tile([P, 1024], F32, name="s_v", tag="s_v", bufs=1)
+            for b in (2 * p, 2 * p + 1):
+                nc.vector.tensor_tensor(
+                    out=heads(half(s_v, b)), in0=heads(acc[b][:])[:, :, :, ::-1], in1=table(sin2, b), op=MULT
+                )
+            o_sb = ring.tile([P, 1024], F32, name="o_sb", tag="o_sb", bufs=4)
+            nc.vector.tensor_tensor(out=o_sb[:], in0=a_sb[p][:], in1=s_v[:], op=ADD)
+            store_pair(p, o_sb[:])
 
-        def plain_out(b, on_scalar):
-            o_sb = ring.tile([P, 512], F32, name="o_sb", tag="o_sb", bufs=8)
-            if on_scalar:
-                nc.scalar.copy(out=o_sb[:], in_=acc[b][:])
-            else:
-                nc.vector.tensor_copy(out=o_sb[:], in_=acc[b][:])
-            store(b, o_sb[:])
+        def plain_out(b):
+            v_sb = ring.tile([P, 512], F32, name="v_sb", tag="v_sb", bufs=4)
+            nc.scalar.copy(out=v_sb[:], in_=acc[b][:])
+            store(b, v_sb[:])
 
         cast(0)
         cast(1)
@@ -231,55 +266,55 @@ def tile_causalselfattention_pa_kernel(
         transposes(0, 0)
         transposes(0, 1)
         for s in range(UNITS):
-            b = s - LAG
-            early = 0 <= b < ROPE_BANKS - 2
+            k = s // 2
+            b = s - PE_LAG
+            p = k - PAIR_LAG
+            if s % 2 == 0:
+                scale_half(s, 0)
+                if k >= 1:
+                    quant(k - 1)
+                if 1 <= s <= 4:
+                    x_quant(s - 1)
+                if p >= 0:
+                    rope_cos(2 * p)
+                    rope_sin(p, k)
+                scale_half(s, 1)
+            else:
+                if p >= 0:
+                    rope_cos(2 * p + 1)
+                    rope_add(p)
+                scale_half(s, 0)
+                if 1 <= s <= 4:
+                    x_quant(s - 1)
+                scale_half(s, 1)
             if s < 4:
                 x_transposes(s)
-            if early:
+            if b >= 0:
                 new_bank(b, "acc")
             for h in range(2):
-                if early:
-                    passes(b, (2 * h, 2 * h + 1))
                 if s + 1 < UNITS:
                     transposes(s + 1, h)
+                if b >= 0:
+                    passes(b, (2 * h, 2 * h + 1))
+            if s >= UNITS - 2:
+                for m in (2 * (s % 2), 2 * (s % 2) + 1):
+                    new_bank(ROPE_BANKS + m, "acc" if m < 2 else "tp")
+                    passes(ROPE_BANKS + m, (0, 1))
             if s < 4:
                 x_out(s, 0)
                 x_out(s, 1)
-            if early:
-                copy_u(b)
             lead = 2 if s < 4 else 3
             while casts_done <= min(s + lead, UNITS - 1):
                 cast(casts_done)
                 casts_done += 1
-            scale_half(s, 0)
-            if s >= 1:
-                quant(s - 1)
-            if 1 <= s <= 4:
-                x_quant(s - 1)
-            if 0 <= b and s < UNITS - 1:
-                rope_cos(b)
-            scale_half(s, 1)
-            if s == UNITS - 1:
-                quant(s)
-                rope_cos(b)
-            if 0 <= b:
-                rope_sin(b)
-                rope_add(b, nc.gpsimd)
-            if s == UNITS - 2:
-                for bb in (ROPE_BANKS - 2, ROPE_BANKS - 1):
-                    new_bank(bb, "acc")
-                    passes(bb, (0, 1, 2, 3))
-                copy_u(ROPE_BANKS - 2)
-                for m in range(4):
-                    new_bank(ROPE_BANKS + m, "acc" if m < 2 else "tp")
-                    passes(ROPE_BANKS + m, (0, 1))
-            if s == UNITS - 1:
-                for m in range(4):
-                    passes(ROPE_BANKS + m, (2,))
+            if 0 <= b < ROPE_BANKS - 2:
+                copy_u(b)
+        last = ROPE_BANKS // 2 - 1
+        rope_cos(2 * last)
+        quant(UNITS // 2 - 1)
         for m in range(4):
-            passes(ROPE_BANKS + m, (3,))
-        rope_cos(ROPE_BANKS - 1)
-        rope_sin_on_vector(ROPE_BANKS - 1)
+            passes(ROPE_BANKS + m, (2, 3))
+        rope_cos(2 * last + 1)
+        rope_rest_on_vector(last)
         for m in range(4):
-            plain_out(ROPE_BANKS + m, True)
-        rope_add(ROPE_BANKS - 1, nc.vector)
+            plain_out(ROPE_BANKS + m)

@@ -57,7 +57,14 @@ def tile_causalselfattention_pa_kernel(
         make_identity(nc, ident[:])
 
         wq = {}
+        wq0 = {}
         xs = {}
+
+        def load_w0(h):
+            wq0[h] = const.tile([P, 2, 512], U8, name="wq0_%d" % h)
+            nc.sync.dma_start(
+                out=wq0[h][:], in_=w_qkv_bytes[256 * h : 256 * (h + 1), 0:512].rearrange("(a p) k -> p a k", p=P)
+            )
 
         def load_w(j):
             i, g = j // 4, j % 4
@@ -76,7 +83,8 @@ def tile_causalselfattention_pa_kernel(
                 in_=x_rows[:, 512 * g : 512 * (g + 1)].rearrange("(m p) k -> p m k", p=P),
             )
 
-        load_w(0)
+        load_w0(0)
+        load_w0(1)
         load_w(1)
         for g in range(4):
             load_x(g)
@@ -86,20 +94,34 @@ def tile_causalselfattention_pa_kernel(
 
         cos2 = const.tile([P, 2, 64, 2], F32, name="cos2")
         sin2 = const.tile([P, 2, 64, 2], F32, name="sin2")
-        nc.gpsimd.tensor_copy(out=cos2[:, :, :, 0], in_=cos_raw[:])
-        nc.gpsimd.tensor_copy(out=cos2[:, :, :, 1], in_=cos_raw[:])
-        nc.gpsimd.tensor_scalar(out=sin2[:, :, :, 0], in0=sin_raw[:], scalar1=-1.0, scalar2=None, op0=MULT)
-        nc.gpsimd.tensor_copy(out=sin2[:, :, :, 1], in_=sin_raw[:])
-
         sin_full = const.tile([P, 1024], F32, name="sin_full")
-        nc.gpsimd.tensor_scalar(
-            out=sin_full[:].rearrange("p (t h n) -> p t h n", t=2, h=4),
-            in0=sin2[:].rearrange("p t j e -> p t (j e)").unsqueeze(2).to_broadcast([P, 2, 4, 128]),
-            scalar1=1.0,
-            scalar2=0.0,
-            op0=MULT,
-            op1=ADD,
-        )
+        sign = const.tile([P, 2], F32, name="sign")
+
+        def tables():
+            nc.vector.memset(sign[:, 0:1], -1.0)
+            nc.vector.memset(sign[:, 1:2], 1.0)
+            nc.gpsimd.tensor_tensor(
+                out=sin2[:].rearrange("p t j e -> p (t j) e"),
+                in0=sin_raw[:].rearrange("p t j -> p (t j)").unsqueeze(2).to_broadcast([P, 128, 2]),
+                in1=sign[:].unsqueeze(1).to_broadcast([P, 128, 2]),
+                op=MULT,
+            )
+            nc.gpsimd.tensor_scalar(
+                out=cos2[:].rearrange("p t j e -> p (t j) e"),
+                in0=cos_raw[:].rearrange("p t j -> p (t j)").unsqueeze(2).to_broadcast([P, 128, 2]),
+                scalar1=1.0,
+                scalar2=0.0,
+                op0=MULT,
+                op1=ADD,
+            )
+            nc.gpsimd.tensor_scalar(
+                out=sin_full[:].rearrange("p (t h n) -> p t h n", t=2, h=4),
+                in0=sin2[:].rearrange("p t j e -> p t (j e)").unsqueeze(2).to_broadcast([P, 2, 4, 128]),
+                scalar1=1.0,
+                scalar2=0.0,
+                op0=MULT,
+                op1=ADD,
+            )
 
         xg = [const.tile([P, 2048], BF16, name="xg%d" % g, align_bytes=64) for g in range(4)]
         xc = [const.tile([P, 512], U32, name="xc%d" % g, align_bytes=64) for g in range(4)]
@@ -116,6 +138,18 @@ def tile_causalselfattention_pa_kernel(
         a_sb = {}
         s_sb = {}
 
+        def cast0():
+            wb[0] = ring.tile([P, 2048], BF16, name="wb", tag="wb", bufs=6)
+            for a in range(2):
+                nc.scalar.copy(out=wb[0][:, 512 * a : 512 * (a + 1)], in_=wq0[0][:, a, :].bitcast(FP8))
+            nc.vector.tensor_copy(out=wb[0][:, 1024:2048], in_=wq0[1][:].rearrange("p a k -> p (a k)").bitcast(FP8))
+
+        def cast1():
+            wb[1] = ring.tile([P, 2048], BF16, name="wb", tag="wb", bufs=6)
+            flat = wq[1][:].rearrange("p a k -> p (a k)")
+            nc.vector.tensor_copy(out=wb[1][:, 0:1024], in_=flat[:, 0:1024].bitcast(FP8))
+            nc.scalar.copy(out=wb[1][:, 1024:2048], in_=flat[:, 1024:2048].bitcast(FP8))
+
         def cast(j):
             wb[j] = ring.tile([P, 2048], BF16, name="wb", tag="wb", bufs=6)
             flat = wq[j][:].rearrange("p a k -> p (a k)")
@@ -126,8 +160,8 @@ def tile_causalselfattention_pa_kernel(
                 )
 
         def turn(words, bank, h):
-            for u in range(2):
-                for a2 in range(2):
+            for a2 in range(2):
+                for u in range(2):
                     a = 2 * h + a2
                     nc.tensor.transpose(
                         bank[:, u, 128 * a2 : 128 * (a2 + 1)],
@@ -252,16 +286,18 @@ def tile_causalselfattention_pa_kernel(
                     out=heads(half(s_v, b)), in0=heads(acc[b][:])[:, :, :, ::-1], in1=table(sin2, b), op=MULT
                 )
             o_sb = ring.tile([P, 1024], F32, name="o_sb", tag="o_sb", bufs=4)
-            nc.vector.tensor_tensor(out=o_sb[:], in0=a_sb[p][:], in1=s_v[:], op=ADD)
-            store_pair(p, o_sb[:])
+            for b in (2 * p, 2 * p + 1):
+                nc.vector.tensor_tensor(out=half(o_sb, b), in0=half(a_sb[p], b), in1=half(s_v, b), op=ADD)
+                store(b, half(o_sb, b))
 
         def plain_out(b):
             v_sb = ring.tile([P, 512], F32, name="v_sb", tag="v_sb", bufs=4)
             nc.scalar.copy(out=v_sb[:], in_=acc[b][:])
             store(b, v_sb[:])
 
-        cast(0)
-        cast(1)
+        cast0()
+        cast1()
+        tables()
         casts_done = 2
         transposes(0, 0)
         transposes(0, 1)

@@ -76,20 +76,18 @@ def tile_causalselfattention_pa_kernel(
                 ),
             )
 
-        def load_x(g):
-            xs[g] = const.tile([P, 4, 512], BF16, name="xs%d" % g)
-            nc.sync.dma_start(
-                out=xs[g][:],
-                in_=x_rows[:, 512 * g : 512 * (g + 1)].rearrange("(m p) k -> p m k", p=P),
-            )
+        def load_x(m):
+            xs[m] = const.tile([P, 2048], BF16, name="xs%d" % m)
+            nc.sync.dma_start(out=xs[m][:], in_=x_rows[128 * m : 128 * (m + 1), :])
 
         load_w0(0)
         load_w0(1)
         load_w(1)
-        for g in range(4):
-            load_x(g)
-            load_w(g + 2)
-        for j in range(6, UNITS):
+        load_w(2)
+        for m in range(4):
+            load_x(m)
+            load_w(m + 3)
+        for j in range(7, UNITS):
             load_w(j)
 
         cos2 = const.tile([P, 2, 64, 2], F32, name="cos2")
@@ -123,9 +121,9 @@ def tile_causalselfattention_pa_kernel(
                 op1=ADD,
             )
 
-        xg = [const.tile([P, 2048], BF16, name="xg%d" % g, align_bytes=64) for g in range(4)]
-        xc = [const.tile([P, 512], U32, name="xc%d" % g, align_bytes=64) for g in range(4)]
-        xsc = [const.tile([P, 512], U8, name="xsc%d" % g, align_bytes=64) for g in range(4)]
+        xg = [const.tile([P, 2048], BF16, name="xg%d" % m, align_bytes=64) for m in range(4)]
+        xc = [const.tile([P, 512], U32, name="xc%d" % m, align_bytes=64) for m in range(4)]
+        xsc = [const.tile([P, 512], U8, name="xsc%d" % m, align_bytes=64) for m in range(4)]
 
         wb = {}
         tp = {}
@@ -173,20 +171,22 @@ def tile_causalselfattention_pa_kernel(
             tp[(j, h)] = psum.tile([P, 2, 256], F32, name="tp", tag="tp")
             turn(wb[j][:].bitcast(F32), tp[(j, h)], h)
 
-        def x_transposes(g):
-            words = xs[g][:].rearrange("p m k -> p (m k)").bitcast(F32)
-            for h in range(2):
-                xt[(g, h)] = psum.tile([P, 2, 256], F32, name="xt", tag="acc")
-                turn(words, xt[(g, h)], h)
+        def x_transposes(m, h):
+            words = xs[m][:].bitcast(F32)
+            xt[(m, h)] = psum.tile([P, 2, 2, 128], F32, name="xt", tag="acc")
+            for g2 in range(2):
+                g = 2 * h + g2
+                for u in range(2):
+                    nc.tensor.transpose(xt[(m, h)][:, g2, u, :], words[:, 256 * g + u : 256 * (g + 1) : 2], ident[:])
 
-        def x_out(g, h):
+        def x_out(m, h):
             nc.scalar.copy(
-                out=xg[g][:, 1024 * h : 1024 * (h + 1)].bitcast(F32).rearrange("p (r u) -> p r u", u=2),
-                in_=xt[(g, h)][:].rearrange("p u r -> p r u"),
+                out=xg[m][:, 1024 * h : 1024 * (h + 1)].bitcast(F32).rearrange("p (g r u) -> p g r u", g=2, u=2),
+                in_=xt[(m, h)][:].rearrange("p g u r -> p g r u"),
             )
 
-        def x_quant(g):
-            nc.vector.quantize_mx(out=xc[g][:].bitcast(FP8X4), scales=xsc[g][:], in_=xg[g][:])
+        def x_quant(m):
+            nc.vector.quantize_mx(out=xc[m][:].bitcast(FP8X4), scales=xsc[m][:], in_=xg[m][:])
 
         def scale_half(j, h):
             g = j % 4
@@ -221,8 +221,8 @@ def tile_causalselfattention_pa_kernel(
                 cols = slice(512 * (j % 2), 512 * (j % 2 + 1))
                 nc.tensor.matmul_mx(
                     out=acc[b][:],
-                    lhsT=xc[g][:, 128 * m : 128 * (m + 1)].bitcast(FP8X4),
-                    lhsT_scale=xsc[g][:, 128 * m : 128 * (m + 1)],
+                    lhsT=xc[m][:, 128 * g : 128 * (g + 1)].bitcast(FP8X4),
+                    lhsT_scale=xsc[m][:, 128 * g : 128 * (g + 1)],
                     rhs=wc[j // 2][:, cols].bitcast(FP8X4),
                     rhs_scale=ws[j // 2][:, cols],
                     start=(g == 0),
@@ -307,10 +307,10 @@ def tile_causalselfattention_pa_kernel(
             p = k - PAIR_LAG
             if s % 2 == 0:
                 scale_half(s, 0)
+                if 3 <= s <= 6:
+                    x_quant(s - 3)
                 if k >= 1:
                     quant(k - 1)
-                if 1 <= s <= 4:
-                    x_quant(s - 1)
                 if p >= 0:
                     rope_cos(2 * p)
                     rope_sin(p, k)
@@ -320,11 +320,12 @@ def tile_causalselfattention_pa_kernel(
                     rope_cos(2 * p + 1)
                     rope_add(p)
                 scale_half(s, 0)
-                if 1 <= s <= 4:
-                    x_quant(s - 1)
+                if 3 <= s <= 6:
+                    x_quant(s - 3)
                 scale_half(s, 1)
-            if s < 4:
-                x_transposes(s)
+            x_banks = [(m, h) for m in range(4) for h in range(2) if m + 1 + h == s]
+            for m, h in x_banks:
+                x_transposes(m, h)
             if b >= 0:
                 new_bank(b, "acc")
             for h in range(2):
@@ -336,9 +337,8 @@ def tile_causalselfattention_pa_kernel(
                 for m in (2 * (s % 2), 2 * (s % 2) + 1):
                     new_bank(ROPE_BANKS + m, "acc" if m < 2 else "tp")
                     passes(ROPE_BANKS + m, (0, 1))
-            if s < 4:
-                x_out(s, 0)
-                x_out(s, 1)
+            for m, h in x_banks:
+                x_out(m, h)
             lead = 2 if s < 4 else 3
             while casts_done <= min(s + lead, UNITS - 1):
                 cast(casts_done)

@@ -11,6 +11,7 @@ U32 = mybir.dt.uint32
 U8 = mybir.dt.uint8
 FP8 = mybir.dt.float8_e4m3fn
 FP8X4 = mybir.dt.float8_e4m3fn_x4
+COPY = mybir.ActivationFunctionType.Copy
 MULT = mybir.AluOpType.mult
 ADD = mybir.AluOpType.add
 
@@ -19,6 +20,8 @@ UNITS = 24
 ROPE_BANKS = 20
 PE_LAG = 4
 PAIR_LAG = 3
+S_UNITS = (23,)
+EARLY = 3
 
 
 def tile_causalselfattention_pa_kernel(
@@ -191,7 +194,7 @@ def tile_causalselfattention_pa_kernel(
         def scale_half(j, h):
             g = j % 4
             k, q = j // 2, j % 2
-            if q == 0 and h == 0:
+            if q == 0 and h == 0 and j + 1 not in S_UNITS:
                 wg[k] = ring.tile([P, 4096], BF16, name="wg", tag="wg%d" % (k % 3), bufs=1, align_bytes=64)
             c0 = 2048 * q + 1024 * h
             nc.vector.tensor_tensor(
@@ -205,6 +208,31 @@ def tile_causalselfattention_pa_kernel(
                 .to_broadcast([P, 256, 2, 2]),
                 op=MULT,
             )
+
+        def scale_on_scalar(j):
+            g = j % 4
+            k, q = j // 2, j % 2
+            wg[k] = ring.tile([P, 4096], BF16, name="wg", tag="wg%d" % (k % 3), bufs=1, align_bytes=64)
+            planes = ring.tile([P, 4, 512], BF16, name="planes", tag="planes", bufs=1)
+            for h in range(2):
+                bank = (
+                    tp[(j, h)][:]
+                    .rearrange("p u r -> p (u r)")
+                    .bitcast(BF16)
+                    .rearrange("p (u r e) -> p u e r", u=2, e=2)
+                )
+                for t in range(4):
+                    nc.scalar.activation(
+                        out=planes[:, t, 256 * h : 256 * (h + 1)],
+                        in_=bank[:, t // 2, t % 2, :],
+                        func=COPY,
+                        scale=scale_sb[:, 4 * g + t : 4 * g + t + 1],
+                    )
+                c0 = 2048 * q + 1024 * h
+                nc.scalar.copy(
+                    out=wg[k][:, c0 : c0 + 1024].rearrange("p (r t) -> p r t", t=4),
+                    in_=planes[:, :, 256 * h : 256 * (h + 1)].rearrange("p t r -> p r t"),
+                )
 
         def quant(k):
             wc[k] = ring.tile([P, 1024], U32, name="wc", tag="wc", bufs=4, align_bytes=64)
@@ -274,9 +302,9 @@ def tile_causalselfattention_pa_kernel(
                 out=pairs(s_sb[p][:]), in0=pairs(u_sb[p][:])[:, :, ::-1], in1=pairs(sin_full[:]), op=MULT
             )
 
-        def rope_add(p):
+        def rope_add(p, eng):
             o_sb = ring.tile([P, 1024], F32, name="o_sb", tag="o_sb", bufs=4)
-            nc.gpsimd.tensor_tensor(out=o_sb[:], in0=a_sb[p][:], in1=s_sb[p][:], op=ADD)
+            eng.tensor_tensor(out=o_sb[:], in0=a_sb[p][:], in1=s_sb[p][:], op=ADD)
             store_pair(p, o_sb[:])
 
         def rope_rest_on_vector(p):
@@ -298,7 +326,6 @@ def tile_causalselfattention_pa_kernel(
         cast0()
         cast1()
         tables()
-        casts_done = 2
         transposes(0, 0)
         transposes(0, 1)
         for s in range(UNITS):
@@ -309,6 +336,8 @@ def tile_causalselfattention_pa_kernel(
                 scale_half(s, 0)
                 if 3 <= s <= 6:
                     x_quant(s - 3)
+                if s - 1 in S_UNITS:
+                    rope_add(p - 1, nc.vector)
                 if k >= 1:
                     quant(k - 1)
                 if p >= 0:
@@ -318,21 +347,26 @@ def tile_causalselfattention_pa_kernel(
             else:
                 if p >= 0:
                     rope_cos(2 * p + 1)
-                    rope_add(p)
-                scale_half(s, 0)
-                if 3 <= s <= 6:
-                    x_quant(s - 3)
-                scale_half(s, 1)
+                if s not in S_UNITS:
+                    if p >= 0:
+                        rope_add(p, nc.gpsimd)
+                    scale_half(s, 0)
+                    if 3 <= s <= 6:
+                        x_quant(s - 3)
+                    scale_half(s, 1)
             x_banks = [(m, h) for m in range(4) for h in range(2) if m + 1 + h == s]
             for m, h in x_banks:
                 x_transposes(m, h)
             if b >= 0:
                 new_bank(b, "acc")
             for h in range(2):
-                if s + 1 < UNITS:
+                if s + 1 < UNITS and s + 1 not in S_UNITS:
                     transposes(s + 1, h)
                 if b >= 0:
                     passes(b, (2 * h, 2 * h + 1))
+            if s + 1 + EARLY in S_UNITS:
+                transposes(s + 1 + EARLY, 0)
+                transposes(s + 1 + EARLY, 1)
             if s >= UNITS - 2:
                 for m in (2 * (s % 2), 2 * (s % 2) + 1):
                     new_bank(ROPE_BANKS + m, "acc" if m < 2 else "tp")
@@ -340,13 +374,16 @@ def tile_causalselfattention_pa_kernel(
             for m, h in x_banks:
                 x_out(m, h)
             lead = 2 if s < 4 else 3
-            while casts_done <= min(s + lead, UNITS - 1):
-                cast(casts_done)
-                casts_done += 1
+            for j in range(UNITS):
+                if j not in wb and (j <= s + lead or (j in S_UNITS and j <= s + 2 + EARLY)):
+                    cast(j)
             if 0 <= b < ROPE_BANKS - 2:
                 copy_u(b)
+            if s + 1 + EARLY in S_UNITS:
+                scale_on_scalar(s + 1 + EARLY)
         last = ROPE_BANKS // 2 - 1
         rope_cos(2 * last)
+        rope_add(last - 1, nc.vector)
         quant(UNITS // 2 - 1)
         for m in range(4):
             passes(ROPE_BANKS + m, (2, 3))

@@ -20,8 +20,8 @@ UNITS = 24
 ROPE_BANKS = 20
 PE_LAG = 4
 PAIR_LAG = 3
-S_UNITS = (23,)
-EARLY = 3
+S_SLOT = {21: 18, 23: 21}
+S_UNITS = tuple(S_SLOT)
 
 
 def tile_causalselfattention_pa_kernel(
@@ -194,7 +194,7 @@ def tile_causalselfattention_pa_kernel(
         def scale_half(j, h):
             g = j % 4
             k, q = j // 2, j % 2
-            if q == 0 and h == 0 and j + 1 not in S_UNITS:
+            if k not in wg:
                 wg[k] = ring.tile([P, 4096], BF16, name="wg", tag="wg%d" % (k % 3), bufs=1, align_bytes=64)
             c0 = 2048 * q + 1024 * h
             nc.vector.tensor_tensor(
@@ -212,7 +212,8 @@ def tile_causalselfattention_pa_kernel(
         def scale_on_scalar(j):
             g = j % 4
             k, q = j // 2, j % 2
-            wg[k] = ring.tile([P, 4096], BF16, name="wg", tag="wg%d" % (k % 3), bufs=1, align_bytes=64)
+            if k not in wg:
+                wg[k] = ring.tile([P, 4096], BF16, name="wg", tag="wg%d" % (k % 3), bufs=1, align_bytes=64)
             planes = ring.tile([P, 4, 512], BF16, name="planes", tag="planes", bufs=1)
             for h in range(2):
                 bank = (
@@ -364,23 +365,24 @@ def tile_causalselfattention_pa_kernel(
                     transposes(s + 1, h)
                 if b >= 0:
                     passes(b, (2 * h, 2 * h + 1))
-            if s + 1 + EARLY in S_UNITS:
-                transposes(s + 1 + EARLY, 0)
-                transposes(s + 1 + EARLY, 1)
+            early = [j for j in S_UNITS if S_SLOT[j] == s]
+            for j in early:
+                transposes(j, 0)
+                transposes(j, 1)
             if s >= UNITS - 2:
                 for m in (2 * (s % 2), 2 * (s % 2) + 1):
                     new_bank(ROPE_BANKS + m, "acc" if m < 2 else "tp")
                     passes(ROPE_BANKS + m, (0, 1))
             for m, h in x_banks:
                 x_out(m, h)
-            lead = 2 if s < 4 else 3
+            lead = 2 if s < 4 else (3 if s < 8 else (4 if s < 12 else 5))
             for j in range(UNITS):
-                if j not in wb and (j <= s + lead or (j in S_UNITS and j <= s + 2 + EARLY)):
+                if j not in wb and (j <= s + lead or (j in S_UNITS and S_SLOT[j] == s + 1)):
                     cast(j)
             if 0 <= b < ROPE_BANKS - 2:
                 copy_u(b)
-            if s + 1 + EARLY in S_UNITS:
-                scale_on_scalar(s + 1 + EARLY)
+            for j in early:
+                scale_on_scalar(j)
         last = ROPE_BANKS // 2 - 1
         rope_cos(2 * last)
         rope_add(last - 1, nc.vector)

@@ -153,12 +153,7 @@ def tile_causalselfattention_pa_kernel(
 
         def cast(j):
             wb[j] = ring.tile([P, 2048], BF16, name="wb", tag="wb", bufs=6)
-            flat = wq[j][:].rearrange("p a k -> p (a k)")
-            for h in range(2):
-                nc.scalar.copy(
-                    out=wb[j][:, 1024 * h : 1024 * (h + 1)],
-                    in_=flat[:, 1024 * h : 1024 * (h + 1)].bitcast(FP8),
-                )
+            nc.scalar.copy(out=wb[j][:], in_=wq[j][:].rearrange("p a k -> p (a k)").bitcast(FP8))
 
         def turn(words, bank, h):
             for a2 in range(2):
@@ -173,6 +168,17 @@ def tile_causalselfattention_pa_kernel(
         def transposes(j, h):
             tp[(j, h)] = psum.tile([P, 2, 256], F32, name="tp", tag="tp")
             turn(wb[j][:].bitcast(F32), tp[(j, h)], h)
+
+        def transposes_by_u(j):
+            words = wb[j][:].bitcast(F32)
+            for u in range(2):
+                tp[(j, u)] = psum.tile([P, 2, 256], F32, name="tp", tag="tp")
+                for a in range(4):
+                    nc.tensor.transpose(
+                        tp[(j, u)][:].rearrange("p u r -> p (u r)")[:, 128 * a : 128 * (a + 1)],
+                        words[:, 256 * a + u : 256 * (a + 1) : 2],
+                        ident[:],
+                    )
 
         def x_transposes(m, h):
             words = xs[m][:].bitcast(F32)
@@ -215,25 +221,17 @@ def tile_causalselfattention_pa_kernel(
             if k not in wg:
                 wg[k] = ring.tile([P, 4096], BF16, name="wg", tag="wg%d" % (k % 3), bufs=1, align_bytes=64)
             planes = ring.tile([P, 4, 512], BF16, name="planes", tag="planes", bufs=1)
-            for h in range(2):
-                bank = (
-                    tp[(j, h)][:]
-                    .rearrange("p u r -> p (u r)")
-                    .bitcast(BF16)
-                    .rearrange("p (u r e) -> p u e r", u=2, e=2)
-                )
-                for t in range(4):
+            for u in range(2):
+                bank = tp[(j, u)][:].rearrange("p u r -> p (u r)").bitcast(BF16).rearrange("p (r e) -> p e r", e=2)
+                for e in range(2):
+                    t = 2 * u + e
                     nc.scalar.activation(
-                        out=planes[:, t, 256 * h : 256 * (h + 1)],
-                        in_=bank[:, t // 2, t % 2, :],
-                        func=COPY,
-                        scale=scale_sb[:, 4 * g + t : 4 * g + t + 1],
+                        out=planes[:, t, :], in_=bank[:, e, :], func=COPY, scale=scale_sb[:, 4 * g + t : 4 * g + t + 1]
                     )
-                c0 = 2048 * q + 1024 * h
-                nc.scalar.copy(
-                    out=wg[k][:, c0 : c0 + 1024].rearrange("p (r t) -> p r t", t=4),
-                    in_=planes[:, :, 256 * h : 256 * (h + 1)].rearrange("p t r -> p r t"),
-                )
+            nc.scalar.copy(
+                out=wg[k][:, 2048 * q : 2048 * (q + 1)].rearrange("p (r t) -> p r t", t=4),
+                in_=planes[:].rearrange("p t r -> p r t"),
+            )
 
         def quant(k):
             wc[k] = ring.tile([P, 1024], U32, name="wc", tag="wc", bufs=4, align_bytes=64)
@@ -367,8 +365,7 @@ def tile_causalselfattention_pa_kernel(
                     passes(b, (2 * h, 2 * h + 1))
             early = [j for j in S_UNITS if S_SLOT[j] == s]
             for j in early:
-                transposes(j, 0)
-                transposes(j, 1)
+                transposes_by_u(j)
             if s >= UNITS - 2:
                 for m in (2 * (s % 2), 2 * (s % 2) + 1):
                     new_bank(ROPE_BANKS + m, "acc" if m < 2 else "tp")

@@ -138,6 +138,7 @@ def tile_causalselfattention_pa_kernel(
         u_sb = {}
         a_sb = {}
         s_sb = {}
+        o_last = {}
 
         def cast0():
             wb[0] = ring.tile([P, 2048], BF16, name="wb", tag="wb", bufs=6)
@@ -306,16 +307,18 @@ def tile_causalselfattention_pa_kernel(
             eng.tensor_tensor(out=o_sb[:], in0=a_sb[p][:], in1=s_sb[p][:], op=ADD)
             store_pair(p, o_sb[:])
 
-        def rope_rest_on_vector(p):
-            s_v = ring.tile([P, 1024], F32, name="s_v", tag="s_v", bufs=1)
+        def rope_sin_on_vector(p):
+            s_sb[p] = ring.tile([P, 1024], F32, name="s_v", tag="s_v", bufs=1)
             for b in (2 * p, 2 * p + 1):
                 nc.vector.tensor_tensor(
-                    out=heads(half(s_v, b)), in0=heads(acc[b][:])[:, :, :, ::-1], in1=table(sin2, b), op=MULT
+                    out=heads(half(s_sb[p], b)), in0=heads(acc[b][:])[:, :, :, ::-1], in1=table(sin2, b), op=MULT
                 )
-            o_sb = ring.tile([P, 1024], F32, name="o_sb", tag="o_sb", bufs=4)
-            for b in (2 * p, 2 * p + 1):
-                nc.vector.tensor_tensor(out=half(o_sb, b), in0=half(a_sb[p], b), in1=half(s_v, b), op=ADD)
-                store(b, half(o_sb, b))
+            o_last[p] = ring.tile([P, 1024], F32, name="o_sb", tag="o_sb", bufs=4)
+
+        def rope_add_bank(b):
+            p = b // 2
+            nc.vector.tensor_tensor(out=half(o_last[p], b), in0=half(a_sb[p], b), in1=half(s_sb[p], b), op=ADD)
+            store(b, half(o_last[p], b))
 
         def plain_out(b):
             v_sb = ring.tile([P, 512], F32, name="v_sb", tag="v_sb", bufs=4)
@@ -387,6 +390,10 @@ def tile_causalselfattention_pa_kernel(
         for m in range(4):
             passes(ROPE_BANKS + m, (2, 3))
         rope_cos(2 * last + 1)
-        rope_rest_on_vector(last)
-        for m in range(4):
-            plain_out(ROPE_BANKS + m)
+        rope_sin_on_vector(last)
+        plain_out(ROPE_BANKS)
+        plain_out(ROPE_BANKS + 1)
+        rope_add_bank(2 * last)
+        plain_out(ROPE_BANKS + 2)
+        rope_add_bank(2 * last + 1)
+        plain_out(ROPE_BANKS + 3)

from contextlib import ExitStack

import concourse.mybir as mybir
from concourse.masks import make_identity

FLOPS = 2 * 512 * 2048 * 3072

F32 = mybir.dt.float32
BF16 = mybir.dt.bfloat16
U32 = mybir.dt.uint32
U8 = mybir.dt.uint8
FP8 = mybir.dt.float8_e4m3fn
FP8X4 = mybir.dt.float8_e4m3fn_x4
COPY = mybir.ActivationFunctionType.Copy
MULT = mybir.AluOpType.mult
ADD = mybir.AluOpType.add

P = 128
UNITS = 24
ROPE_BANKS = 20
PE_LAG = 4
PAIR_LAG = 3
S_SLOT = {21: 18, 23: 21}
S_UNITS = tuple(S_SLOT)


def tile_causalselfattention_pa_kernel(
    tc, x, w_qkv_bytes, w_qkv_scale, freqs_cos, freqs_sin, out_0, out_1, out_2
):
    nc = tc.nc
    x_rows = x.flatten_outer_dims()
    out_rows = [
        out_0.rearrange("b t h d -> (b t) (h d)"),
        out_1.rearrange("b t h d -> (b t) (h d)"),
        out_2.rearrange("b t h d -> (b t) (h d)"),
    ]

    with ExitStack() as ctx:
        const = ctx.enter_context(tc.tile_pool(name="const", bufs=1))
        ring = ctx.enter_context(tc.tile_pool(name="ring", bufs=4))
        psum = ctx.enter_context(tc.psum_pool(name="psum", bufs=4))
        ctx.enter_context(tc.manual_schedule())

        scale_sb = const.tile([P, 16], F32, name="scale_sb")
        nc.scalar.dma_start(
            out=scale_sb[:].rearrange("p (g t) -> p g t", t=4),
            in_=w_qkv_scale.rearrange("o (g p t) -> p (o g) t", p=P, t=4),
        )
        cos_raw = const.tile([P, 2, 64], BF16, name="cos_raw")
        nc.scalar.dma_start(out=cos_raw[:], in_=freqs_cos.rearrange("(th p) j -> p th j", p=P))
        sin_raw = const.tile([P, 2, 64], BF16, name="sin_raw")
        nc.scalar.dma_start(out=sin_raw[:], in_=freqs_sin.rearrange("(th p) j -> p th j", p=P))

        warm_in = const.tile([P, 1], F32, name="warm_in")
        warm_out = const.tile([P, 1], F32, name="warm_out")
        nc.gpsimd.memset(warm_in[:], 0.0)
        nc.scalar.copy(out=warm_out[:], in_=warm_in[:])

        ident = const.tile([P, P], F32, name="ident")
        make_identity(nc, ident[:])

        wq = {}
        wq0 = {}
        xs = {}

        def load_w0(h):
            wq0[h] = const.tile([P, 2, 512], U8, name="wq0_%d" % h)
            nc.sync.dma_start(
                out=wq0[h][:], in_=w_qkv_bytes[256 * h : 256 * (h + 1), 0:512].rearrange("(a p) k -> p a k", p=P)
            )

        def load_w(j):
            i, g = j // 4, j % 4
            wq[j] = const.tile([P, 4, 512], U8, name="wq%d" % j)
            nc.sync.dma_start(
                out=wq[j][:],
                in_=w_qkv_bytes[512 * i : 512 * (i + 1), 512 * g : 512 * (g + 1)].rearrange(
                    "(a p) k -> p a k", p=P
                ),
            )

        def load_x(m):
            xs[m] = const.tile([P, 2048], BF16, name="xs%d" % m)
            nc.sync.dma_start(out=xs[m][:], in_=x_rows[128 * m : 128 * (m + 1), :])

        load_w0(0)
        load_w0(1)
        load_w(1)
        load_w(2)
        for m in range(4):
            load_x(m)
            load_w(m + 3)
        for j in range(7, UNITS):
            load_w(j)

        cos2 = const.tile([P, 2, 64, 2], F32, name="cos2")
        sin2 = const.tile([P, 2, 64, 2], F32, name="sin2")
        sin_full = const.tile([P, 1024], F32, name="sin_full")
        sign = const.tile([P, 2], F32, name="sign")

        def tables():
            nc.vector.memset(sign[:, 0:1], -1.0)
            nc.vector.memset(sign[:, 1:2], 1.0)
            nc.gpsimd.tensor_tensor(
                out=sin2[:].rearrange("p t j e -> p (t j) e"),
                in0=sin_raw[:].rearrange("p t j -> p (t j)").unsqueeze(2).to_broadcast([P, 128, 2]),
                in1=sign[:].unsqueeze(1).to_broadcast([P, 128, 2]),
                op=MULT,
            )
            nc.gpsimd.tensor_scalar(
                out=cos2[:].rearrange("p t j e -> p (t j) e"),
                in0=cos_raw[:].rearrange("p t j -> p (t j)").unsqueeze(2).to_broadcast([P, 128, 2]),
                scalar1=1.0,
                scalar2=0.0,
                op0=MULT,
                op1=ADD,
            )
            nc.gpsimd.tensor_scalar(
                out=sin_full[:].rearrange("p (t h n) -> p t h n", t=2, h=4),
                in0=sin2[:].rearrange("p t j e -> p t (j e)").unsqueeze(2).to_broadcast([P, 2, 4, 128]),
                scalar1=1.0,
                scalar2=0.0,
                op0=MULT,
                op1=ADD,
            )

        xg = [const.tile([P, 2048], BF16, name="xg%d" % m, align_bytes=64) for m in range(4)]
        xc = [const.tile([P, 512], U32, name="xc%d" % m, align_bytes=64) for m in range(4)]
        xsc = [const.tile([P, 512], U8, name="xsc%d" % m, align_bytes=64) for m in range(4)]

        wb = {}
        tp = {}
        xt = {}
        wg = {}
        wc = {}
        ws = {}
        acc = {}
        u_sb = {}
        a_sb = {}
        s_sb = {}
        o_last = {}

        def cast0():
            wb[0] = ring.tile([P, 2048], BF16, name="wb", tag="wb", bufs=6)
            for a in range(2):
                nc.scalar.copy(out=wb[0][:, 512 * a : 512 * (a + 1)], in_=wq0[0][:, a, :].bitcast(FP8))
            nc.vector.tensor_copy(out=wb[0][:, 1024:2048], in_=wq0[1][:].rearrange("p a k -> p (a k)").bitcast(FP8))

        def cast1():
            wb[1] = ring.tile([P, 2048], BF16, name="wb", tag="wb", bufs=6)
            flat = wq[1][:].rearrange("p a k -> p (a k)")
            nc.vector.tensor_copy(out=wb[1][:, 0:1024], in_=flat[:, 0:1024].bitcast(FP8))
            nc.scalar.copy(out=wb[1][:, 1024:2048], in_=flat[:, 1024:2048].bitcast(FP8))

        def cast(j):
            wb[j] = ring.tile([P, 2048], BF16, name="wb", tag="wb", bufs=6)
            nc.scalar.copy(out=wb[j][:], in_=wq[j][:].rearrange("p a k -> p (a k)").bitcast(FP8))

        def turn(words, bank, h):
            for a2 in range(2):
                for u in range(2):
                    a = 2 * h + a2
                    nc.tensor.transpose(
                        bank[:, u, 128 * a2 : 128 * (a2 + 1)],
                        words[:, 256 * a + u : 256 * (a + 1) : 2],
                        ident[:],
                    )

        def transposes(j, h):
            tp[(j, h)] = psum.tile([P, 2, 256], F32, name="tp", tag="tp")
            turn(wb[j][:].bitcast(F32), tp[(j, h)], h)

        def transposes_by_u(j):
            words = wb[j][:].bitcast(F32)
            for u in range(2):
                tp[(j, u)] = psum.tile([P, 2, 256], F32, name="tp", tag="tp")
                for a in range(4):
                    nc.tensor.transpose(
                        tp[(j, u)][:].rearrange("p u r -> p (u r)")[:, 128 * a : 128 * (a + 1)],
                        words[:, 256 * a + u : 256 * (a + 1) : 2],
                        ident[:],
                    )

        def x_transposes(m, h):
            words = xs[m][:].bitcast(F32)
            xt[(m, h)] = psum.tile([P, 2, 2, 128], F32, name="xt", tag="acc")
            for g2 in range(2):
                g = 2 * h + g2
                for u in range(2):
                    nc.tensor.transpose(xt[(m, h)][:, g2, u, :], words[:, 256 * g + u : 256 * (g + 1) : 2], ident[:])

        def x_out(m, h):
            nc.scalar.copy(
                out=xg[m][:, 1024 * h : 1024 * (h + 1)].bitcast(F32).rearrange("p (g r u) -> p g r u", g=2, u=2),
                in_=xt[(m, h)][:].rearrange("p g u r -> p g r u"),
            )

        def x_quant(m):
            nc.vector.quantize_mx(out=xc[m][:].bitcast(FP8X4), scales=xsc[m][:], in_=xg[m][:])

        def scale_half(j, h):
            g = j % 4
            k, q = j // 2, j % 2
            if k not in wg:
                wg[k] = ring.tile([P, 4096], BF16, name="wg", tag="wg%d" % (k % 3), bufs=1, align_bytes=64)
            c0 = 2048 * q + 1024 * h
            nc.vector.tensor_tensor(
                out=wg[k][:, c0 : c0 + 1024].rearrange("p (r u e) -> p r u e", u=2, e=2),
                in0=tp[(j, h)][:]
                .rearrange("p u r -> p (u r)")
                .bitcast(BF16)
                .rearrange("p (u r e) -> p r u e", u=2, e=2),
                in1=scale_sb[:, 4 * g : 4 * g + 4]
                .rearrange("p (o u e) -> p o u e", o=1, u=2, e=2)
                .to_broadcast([P, 256, 2, 2]),
                op=MULT,
            )

        def scale_on_scalar(j):
            g = j % 4
            k, q = j // 2, j % 2
            if k not in wg:
                wg[k] = ring.tile([P, 4096], BF16, name="wg", tag="wg%d" % (k % 3), bufs=1, align_bytes=64)
            planes = ring.tile([P, 4, 512], BF16, name="planes", tag="planes", bufs=1)
            for u in range(2):
                bank = tp[(j, u)][:].rearrange("p u r -> p (u r)").bitcast(BF16).rearrange("p (r e) -> p e r", e=2)
                for e in range(2):
                    t = 2 * u + e
                    nc.scalar.activation(
                        out=planes[:, t, :], in_=bank[:, e, :], func=COPY, scale=scale_sb[:, 4 * g + t : 4 * g + t + 1]
                    )
            nc.scalar.copy(
                out=wg[k][:, 2048 * q : 2048 * (q + 1)].rearrange("p (r t) -> p r t", t=4),
                in_=planes[:].rearrange("p t r -> p r t"),
            )

        def quant(k):
            wc[k] = ring.tile([P, 1024], U32, name="wc", tag="wc", bufs=4, align_bytes=64)
            ws[k] = ring.tile([P, 1024], U8, name="ws", tag="ws", bufs=4, align_bytes=64)
            nc.vector.quantize_mx(out=wc[k][:].bitcast(FP8X4), scales=ws[k][:], in_=wg[k][:])

        def new_bank(b, tag):
            acc[b] = psum.tile([P, 512], F32, name="acc", tag=tag)

        def passes(b, gs):
            i, m = b // 4, b % 4
            for g in gs:
                j = 4 * i + g
                cols = slice(512 * (j % 2), 512 * (j % 2 + 1))
                nc.tensor.matmul_mx(
                    out=acc[b][:],
                    lhsT=xc[m][:, 128 * g : 128 * (g + 1)].bitcast(FP8X4),
                    lhsT_scale=xsc[m][:, 128 * g : 128 * (g + 1)],
                    rhs=wc[j // 2][:, cols].bitcast(FP8X4),
                    rhs_scale=ws[j // 2][:, cols],
                    start=(g == 0),
                    stop=(g == 3),
                )

        def out_view(b):
            i = b // 4
            dst = out_rows[0] if i < 4 else out_rows[i - 3]
            c0 = 512 * i if i < 4 else 0
            return dst[:, c0 : c0 + 512]

        def store(b, tile_ap):
            m = b % 4
            nc.sync.dma_start(out=out_view(b)[128 * m : 128 * (m + 1), :], in_=tile_ap)

        def store_pair(p, tile_ap):
            m = (2 * p) % 4
            nc.sync.dma_start(
                out=out_view(2 * p)[128 * m : 128 * (m + 2), :].rearrange("(t p) c -> p t c", p=P),
                in_=tile_ap.rearrange("p (t c) -> p t c", t=2),
            )

        def heads(ap):
            return ap.rearrange("p (h j e) -> p h j e", h=4, e=2)

        def pairs(ap):
            return ap.rearrange("p (n e) -> p n e", e=2)

        def table(t, b):
            return t[:, b % 2, :, :].unsqueeze(1).to_broadcast([P, 4, 64, 2])

        def half(t, b):
            return t[:, 512 * (b % 2) : 512 * (b % 2 + 1)]

        def copy_u(b):
            if b % 2 == 0:
                u_sb[b // 2] = ring.tile([P, 1024], F32, name="u_sb", tag="u_sb", bufs=3)
            nc.scalar.copy(out=half(u_sb[b // 2], b), in_=acc[b][:])

        def rope_cos(b):
            if b % 2 == 0:
                a_sb[b // 2] = ring.tile([P, 1024], F32, name="a_sb", tag="a_sb", bufs=3)
            nc.vector.tensor_tensor(out=heads(half(a_sb[b // 2], b)), in0=heads(acc[b][:]), in1=table(cos2, b), op=MULT)

        def rope_sin(p, k):
            s_sb[p] = ring.tile([P, 1024], F32, name="s_sb", tag="wg%d" % ((k - 1) % 3), bufs=1, align_bytes=64)
            nc.gpsimd.tensor_tensor(
                out=pairs(s_sb[p][:]), in0=pairs(u_sb[p][:])[:, :, ::-1], in1=pairs(sin_full[:]), op=MULT
            )

        def rope_add(p, eng):
            o_sb = ring.tile([P, 1024], F32, name="o_sb", tag="o_sb", bufs=4)
            eng.tensor_tensor(out=o_sb[:], in0=a_sb[p][:], in1=s_sb[p][:], op=ADD)
            store_pair(p, o_sb[:])

        def rope_sin_on_vector(p):
            s_sb[p] = ring.tile([P, 1024], F32, name="s_v", tag="s_v", bufs=1)
            for b in (2 * p, 2 * p + 1):
                nc.vector.tensor_tensor(
                    out=heads(half(s_sb[p], b)), in0=heads(acc[b][:])[:, :, :, ::-1], in1=table(sin2, b), op=MULT
                )
            o_last[p] = ring.tile([P, 1024], F32, name="o_sb", tag="o_sb", bufs=4)

        def rope_add_bank(b):
            p = b // 2
            nc.vector.tensor_tensor(out=half(o_last[p], b), in0=half(a_sb[p], b), in1=half(s_sb[p], b), op=ADD)
            store(b, half(o_last[p], b))

        def plain_out(b):
            v_sb = ring.tile([P, 512], F32, name="v_sb", tag="v_sb", bufs=4)
            nc.scalar.copy(out=v_sb[:], in_=acc[b][:])
            store(b, v_sb[:])

        cast0()
        cast1()
        tables()
        transposes(0, 0)
        transposes(0, 1)
        for s in range(UNITS):
            k = s // 2
            b = s - PE_LAG
            p = k - PAIR_LAG
            if s % 2 == 0:
                scale_half(s, 0)
                if 3 <= s <= 6:
                    x_quant(s - 3)
                if s - 1 in S_UNITS:
                    rope_add(p - 1, nc.vector)
                if k >= 1:
                    quant(k - 1)
                if p >= 0:
                    rope_cos(2 * p)
                    rope_sin(p, k)
                scale_half(s, 1)
            else:
                if p >= 0:
                    rope_cos(2 * p + 1)
                if s not in S_UNITS:
                    if p >= 0:
                        rope_add(p, nc.gpsimd)
                    scale_half(s, 0)
                    if 3 <= s <= 6:
                        x_quant(s - 3)
                    scale_half(s, 1)
            x_banks = [(m, h) for m in range(4) for h in range(2) if m + 1 + h == s]
            for m, h in x_banks:
                x_transposes(m, h)
            if b >= 0:
                new_bank(b, "acc")
            for h in range(2):
                if s + 1 < UNITS and s + 1 not in S_UNITS:
                    transposes(s + 1, h)
                if b >= 0:
                    passes(b, (2 * h, 2 * h + 1))
            early = [j for j in S_UNITS if S_SLOT[j] == s]
            for j in early:
                transposes_by_u(j)
            if s >= UNITS - 2:
                for m in (2 * (s % 2), 2 * (s % 2) + 1):
                    new_bank(ROPE_BANKS + m, "acc" if m < 2 else "tp")
                    passes(ROPE_BANKS + m, (0, 1))
            for m, h in x_banks:
                x_out(m, h)
            lead = 2 if s < 4 else (3 if s < 8 else (4 if s < 12 else 5))
            for j in range(UNITS):
                if j not in wb and (j <= s + lead or (j in S_UNITS and S_SLOT[j] == s + 1)):
                    cast(j)
            if 0 <= b < ROPE_BANKS - 2:
                copy_u(b)
            for j in early:
                scale_on_scalar(j)
        last = ROPE_BANKS // 2 - 1
        rope_cos(2 * last)
        rope_add(last - 1, nc.vector)
        quant(UNITS // 2 - 1)
        for m in range(4):
            passes(ROPE_BANKS + m, (2, 3))
        rope_cos(2 * last + 1)
        rope_sin_on_vector(last)
        plain_out(ROPE_BANKS)
        plain_out(ROPE_BANKS + 1)
        rope_add_bank(2 * last)
        plain_out(ROPE_BANKS + 2)
        rope_add_bank(2 * last + 1)
        plain_out(ROPE_BANKS + 3)
